import numpy as np
import ml_dtypes


def mxq(x, axis, fmt="e4m3"):
    dtype, down = {"e4m3": (ml_dtypes.float8_e4m3fn, 7), "e5m2": (ml_dtypes.float8_e5m2, 14)}[fmt]
    v = np.moveaxis(np.asarray(x, np.float32).astype(ml_dtypes.bfloat16).astype(np.float64), axis, -1)
    blocks = v.reshape(v.shape[:-1] + (-1, 32))
    amax = np.abs(blocks).max(-1, keepdims=True)
    byte = np.maximum(np.where(amax > 0, np.frexp(amax)[1] - 1 + 127, 0) - down, 1)
    scale = np.exp2(byte - 127.0)
    codes = (blocks / scale).astype(np.float32).astype(dtype).astype(np.float64)
    return np.moveaxis((codes * scale).reshape(v.shape), -1, axis)


WIDE = False


def mx_kscale(k):
    if not WIDE:
        return np.ones(k)
    levels = np.array([10, -10, 5, -5, 0])
    a = np.random.permutation(np.resize(levels, k // 512 * 4)).reshape(k // 512, 4)
    idx = np.arange(k)
    return np.exp2(a[idx // 512, idx % 128 // 32])


BF16 = ml_dtypes.bfloat16


def bf(x):
    return np.asarray(x, np.float32).astype(BF16)


def f64(x):
    return np.asarray(x).astype(np.float64)


E2M1 = np.array([0.0, 0.5, 1.0, 1.5, 2.0, 3.0, 4.0, 6.0, -0.0, -0.5, -1.0, -1.5, -2.0, -3.0, -4.0, -6.0])


def pack_weight(w, fmt):
    k, n = w.shape
    w = f64(bf(w)).reshape(k // 32, 32, n)
    amax = np.abs(w).max(1)
    if fmt == "e4m3":
        byte = np.frexp(amax)[1] - 1 + 127 - 7
    else:
        mant, ex = np.frexp(amax / 6.0)
        byte = np.where(mant > 0.5, ex, ex - 1) + 127
    byte = np.clip(np.where(amax > 0, byte, 1), 1, 254)
    scaled = (w * np.exp2(127.0 - byte)[:, None, :]).reshape(k, n).astype(np.float32)
    by_word = np.ascontiguousarray(scaled.reshape(k // 512, 128, 4, n).transpose(0, 1, 3, 2))
    if fmt == "e4m3":
        words = by_word.astype(ml_dtypes.float8_e4m3fn).view(np.uint8)
    else:
        c = by_word.astype(ml_dtypes.float4_e2m1fn).view(np.uint8) & 0xF
        words = c[..., 0::2] | (c[..., 1::2] << 4)
    return np.ascontiguousarray(words), np.ascontiguousarray(byte.astype(np.uint8).reshape(k // 512, 16, n))


def unpack_weight(words, scales, fmt):
    g, p, n, _ = words.shape
    if fmt == "e4m3":
        vals = np.ascontiguousarray(words).view(ml_dtypes.float8_e4m3fn).astype(np.float64)
    else:
        nib = np.empty((g, p, n, 4), np.uint8)
        nib[..., 0::2] = words & 0xF
        nib[..., 1::2] = words >> 4
        vals = E2M1[nib]
    vals = vals * np.repeat(np.exp2(scales.astype(np.float64) - 127.0), 8, axis=1)[..., None]
    return vals.transpose(0, 1, 3, 2).reshape(g * 512, n)


B, H, W, C, F, KH, KW = 1024, 3, 2, 512, 1024, 2, 1
OH, OW = H - KH + 1, W - KW + 1
K = KH * KW * C
E = OH * OW
BN_EPS = 1e-3


def extract_patches(x, kh, kw):
    b, h, w, c = x.shape
    oh, ow = h - kh + 1, w - kw + 1
    slices = [x[:, i:i + oh, j:j + ow, :] for i in range(kh) for j in range(kw)]
    return np.stack(slices, axis=3).reshape(b, oh, ow, kh * kw * c)


def setup_inputs():
    s = mx_kscale(C)
    x = bf(np.random.standard_normal((B, H, W, C)) * 0.14)
    gamma = bf((1.0 + 0.1 * np.random.standard_normal(C)) * s)
    beta = bf(0.3 * np.random.standard_normal(C) * s)
    moving_mean = bf(0.05 * np.random.standard_normal(C))
    moving_var = bf(0.01 + 0.02 * np.random.random(C))
    stack = np.random.standard_normal((OH * OW, K, F)) / np.sqrt(K) / np.tile(s, KH * KW)[None, :, None]
    words, scales = pack_weight(stack.reshape(-1, F), "e4m3")
    return {"x": x,
            "gamma": gamma,
            "beta": beta,
            "moving_mean": moving_mean,
            "moving_var": moving_var,
            "weight_words": words,
            "weight_scales": scales}


def reference(x, gamma, beta, moving_mean, moving_var, weight_words, weight_scales):
    inv = f64(gamma) / np.sqrt(f64(moving_var) + BN_EPS)
    xn = (f64(x) - f64(moving_mean)) * inv + f64(beta)
    xq = mxq(xn, 3, "e4m3")
    patches = extract_patches(xq, KH, KW)
    p = patches.reshape(B, OH * OW, K).transpose(1, 0, 2)
    y = p @ unpack_weight(weight_words, weight_scales, "e4m3").reshape(E, K, F)
    y = y.transpose(1, 0, 2).reshape(B, OH, OW, F)
    return np.maximum(y, 0.0)

@@ -1,0 +1,227 @@
+from contextlib import ExitStack
+
+import concourse.mybir as mybir
+from concourse.masks import make_identity
+
+F32 = mybir.dt.float32
+BF16 = mybir.dt.bfloat16
+I32 = mybir.dt.int32
+U32 = mybir.dt.uint32
+U8 = mybir.dt.uint8
+FP8X4 = mybir.dt.float8_e4m3fn_x4
+ACT = mybir.ActivationFunctionType
+ALU = mybir.AluOpType
+
+P = 128
+PACK = 4
+BATCH = 1024
+IN_ROWS = 3
+OUT_ROWS = 2
+WIDTH = 2
+WINDOW = 2
+CHANNELS = P * PACK
+FEATURES = 1024
+BN_EPS = 1e-3
+
+BATCH_TILES = BATCH // P
+ROW_COLS = WIDTH * P
+TILE_COLS = IN_ROWS * ROW_COLS
+WORDS_PER_PIXEL = CHANNELS // 2
+N_HALF = 512
+HALVES = FEATURES // N_HALF
+WEIGHT_GROUPS = OUT_ROWS * WIDTH * WINDOW
+PLANES_PER_TILE = 4
+BANKS_PER_TILE = OUT_ROWS * WIDTH * HALVES
+AHEAD = 2
+
+FLOPS = 2 * BATCH * OUT_ROWS * WIDTH * WINDOW * CHANNELS * FEATURES
+
+
+def tile_blockrf_t_e_kernel(
+    tc, x, gamma, beta, moving_mean, moving_var, weight_words, weight_scales, out
+):
+    nc = tc.nc
+
+    x_dram = x.rearrange("(j p) h w c -> j p (h w c)", p=P)
+    out_dram = out.rearrange("(j p) h w f -> j p h (w f)", p=P)
+    words_dram = weight_words.rearrange("g p n t -> p g (n t)").bitcast(I32)
+    scales_dram = weight_scales.bitcast(I32)
+
+    with ExitStack() as ctx:
+        keep = ctx.enter_context(tc.tile_pool(name="keep", bufs=1))
+        plane_pool = ctx.enter_context(tc.tile_pool(name="planes", bufs=2 * IN_ROWS))
+        grouped_pool = ctx.enter_context(tc.tile_pool(name="grouped", bufs=3))
+        result_pool = ctx.enter_context(tc.tile_pool(name="result", bufs=8))
+        turned_pool = ctx.enter_context(tc.psum_pool(name="turned", bufs=IN_ROWS))
+        acc_pool = ctx.enter_context(tc.psum_pool(name="acc", bufs=8 - IN_ROWS))
+        ctx.enter_context(tc.manual_schedule())
+
+        x_sb = keep.tile([P, BATCH_TILES, IN_ROWS * WIDTH * CHANNELS], BF16)
+        w_words = keep.tile([P, WEIGHT_GROUPS, FEATURES], U32, align_bytes=64)
+        w_planes = keep.tile(
+            [P, WEIGHT_GROUPS // PLANES_PER_TILE, FEATURES], U8, align_bytes=64
+        )
+        x_codes = keep.tile([P, BATCH_TILES, TILE_COLS], U32, align_bytes=64)
+        x_scales = keep.tile([P, BATCH_TILES, TILE_COLS], U8, align_bytes=64)
+        identity = keep.tile([P, P], F32)
+
+        raw = {}
+        for name, vector in (
+            ("var", moving_var),
+            ("gamma", gamma),
+            ("mean", moving_mean),
+            ("beta", beta),
+        ):
+            raw[name] = keep.tile([P, PACK], BF16, name="raw_" + name)
+            nc.scalar.dma_start(out=raw[name][:], in_=vector.rearrange("(p t) -> p t", t=PACK))
+
+        def load_x(j):
+            nc.sync.dma_start(out=x_sb[:, j, :], in_=x_dram[j])
+
+        def load_weight_words(e):
+            groups = slice(WINDOW * e, WINDOW * (e + 1))
+            nc.sync.dma_start(
+                out=w_words[:, groups, :].bitcast(I32), in_=words_dram[:, groups, :]
+            )
+
+        nc.vector.memset(w_planes[:].bitcast(I32), 0)
+        make_identity(nc, identity[:])
+
+        for j in range(AHEAD + 1):
+            load_x(j)
+        load_weight_words(0)
+        for block in range(WEIGHT_GROUPS // PLANES_PER_TILE):
+            groups = slice(PLANES_PER_TILE * block, PLANES_PER_TILE * (block + 1))
+            for quadrant in range(4):
+                nc.sync.dma_start(
+                    out=w_planes[32 * quadrant : 32 * quadrant + 16, block, :].bitcast(I32),
+                    in_=scales_dram[groups, 4 * quadrant : 4 * quadrant + 4, :],
+                )
+        for e in range(1, OUT_ROWS * WIDTH):
+            load_weight_words(e)
+        for j in range(AHEAD + 1, BATCH_TILES):
+            load_x(j)
+
+        def small(name):
+            return keep.tile([P, PACK], F32, name=name)
+
+        var_eps = small("var_eps")
+        nc.vector.tensor_scalar_add(var_eps[:], raw["var"][:], BN_EPS)
+        std = small("std")
+        nc.scalar.activation(out=std[:], in_=var_eps[:], func=ACT.Sqrt)
+        rstd = small("rstd")
+        nc.vector.reciprocal(rstd[:], std[:])
+        r_sq = small("r_sq")
+        nc.vector.tensor_mul(r_sq[:], rstd[:], rstd[:])
+        v_r_sq = small("v_r_sq")
+        nc.vector.tensor_mul(v_r_sq[:], r_sq[:], var_eps[:])
+        factor = small("factor")
+        nc.vector.tensor_scalar(
+            out=factor[:], in0=v_r_sq[:], scalar1=-0.5, scalar2=1.5, op0=ALU.mult, op1=ALU.add
+        )
+        rstd_fine = small("rstd_fine")
+        nc.vector.tensor_mul(rstd_fine[:], rstd[:], factor[:])
+        bn_scale = small("bn_scale")
+        nc.vector.tensor_mul(bn_scale[:], raw["gamma"][:], rstd_fine[:])
+        mean_scaled = small("mean_scaled")
+        nc.vector.tensor_mul(mean_scaled[:], raw["mean"][:], bn_scale[:])
+        bn_shift = small("bn_shift")
+        nc.vector.tensor_sub(bn_shift[:], raw["beta"][:], mean_scaled[:])
+
+        turned = {}
+        planes = {}
+        grouped = {}
+        result = {}
+
+        def transpose_tile(j):
+            x_as_words = x_sb[:, j, :].bitcast(F32)
+            for h in range(IN_ROWS):
+                turned[j, h] = turned_pool.tile([P, 2, ROW_COLS], F32, name="turned")
+                for w in range(WIDTH):
+                    pixel = h * WIDTH + w
+                    for u in range(2):
+                        nc.tensor.transpose(
+                            out=turned[j, h][:, u, w * P : (w + 1) * P],
+                            in_=x_as_words[
+                                :, pixel * WORDS_PER_PIXEL + u : (pixel + 1) * WORDS_PER_PIXEL : 2
+                            ],
+                            identity=identity[:],
+                        )
+
+        def batch_norm(j, h):
+            planes[j, h] = plane_pool.tile([P, PACK, ROW_COLS], BF16, name="planes")
+            halves = turned[j, h][:].bitcast(BF16).rearrange("p u (c e) -> p u c e", e=2)
+            for t in range(PACK):
+                nc.scalar.activation(
+                    out=planes[j, h][:, t, :],
+                    in_=halves[:, t // 2, :, t % 2],
+                    func=ACT.Identity,
+                    scale=bn_scale[:, t : t + 1],
+                    bias=bn_shift[:, t : t + 1],
+                )
+
+        def regroup(j, h):
+            grouped[j, h] = grouped_pool.tile(
+                [P, ROW_COLS, PACK], BF16, name="grouped", align_bytes=64
+            )
+            nc.vector.tensor_copy(
+                out=grouped[j, h][:].rearrange("p (c i) t -> p c t i", i=4),
+                in_=planes[j, h][:].rearrange("p t (c i) -> p c t i", i=4),
+            )
+
+        def quantise(j, h):
+            cols = slice(h * ROW_COLS, (h + 1) * ROW_COLS)
+            nc.vector.quantize_mx(
+                out=x_codes[:, j, cols].bitcast(FP8X4),
+                scales=x_scales[:, j, cols],
+                in_=grouped[j, h][:].rearrange("p c t -> p (c t)"),
+            )
+
+        def quantise_tile(j):
+            for h in range(IN_ROWS + 1):
+                if h < IN_ROWS:
+                    regroup(j, h)
+                if h >= 1:
+                    quantise(j, h - 1)
+
+        def multiply(j, bank):
+            e, half = divmod(bank, HALVES)
+            h, w = divmod(e, WIDTH)
+            f_cols = slice(half * N_HALF, (half + 1) * N_HALF)
+            acc = acc_pool.tile([P, N_HALF], F32, name="acc")
+            for i in range(WINDOW):
+                g = WINDOW * e + i
+                pixel = (h + i) * WIDTH + w
+                b_cols = slice(pixel * P, (pixel + 1) * P)
+                nc.tensor.matmul_mx(
+                    out=acc[:],
+                    lhsT=x_codes[:, j, b_cols].bitcast(FP8X4),
+                    lhsT_scale=x_scales[:, j, b_cols],
+                    rhs=w_words[:, g, f_cols].bitcast(FP8X4),
+                    rhs_scale=w_planes[
+                        4 * (g % PLANES_PER_TILE) : P, g // PLANES_PER_TILE, f_cols
+                    ],
+                    start=(i == 0),
+                    stop=(i == WINDOW - 1),
+                )
+            if w == 0 and half == 0:
+                result[j, h] = result_pool.tile([P, WIDTH, FEATURES], F32, name="result")
+            if bank % 3 == 0:
+                nc.scalar.activation(out=result[j, h][:, w, f_cols], in_=acc[:], func=ACT.Relu)
+            else:
+                nc.vector.tensor_scalar_max(result[j, h][:, w, f_cols], acc[:], 0.0)
+            if w == WIDTH - 1 and half == HALVES - 1:
+                nc.sync.dma_start(
+                    out=out_dram[j, :, h, :], in_=result[j, h][:].rearrange("p w f -> p (w f)")
+                )
+
+        for s in range(BATCH_TILES + AHEAD):
+            if s < BATCH_TILES:
+                transpose_tile(s)
+            if 1 <= s <= BATCH_TILES:
+                quantise_tile(s - 1)
+            for bank in range(BANKS_PER_TILE):
+                if s < BATCH_TILES and bank % 3 == 0:
+                    batch_norm(s, bank // 3)
+                if s >= AHEAD:
+                    multiply(s - AHEAD, bank)

@@ -31,8 +31,7 @@ N_HALF = 512
 HALVES = FEATURES // N_HALF
 WEIGHT_GROUPS = OUT_ROWS * WIDTH * WINDOW
 PLANES_PER_TILE = 4
-BANKS_PER_TILE = OUT_ROWS * WIDTH * HALVES
-AHEAD = 2
+FIRST_TILES = 2
 
 FLOPS = 2 * BATCH * OUT_ROWS * WIDTH * WINDOW * CHANNELS * FEATURES
 
@@ -49,7 +48,7 @@ def tile_blockrf_t_e_kernel(
 
     with ExitStack() as ctx:
         keep = ctx.enter_context(tc.tile_pool(name="keep", bufs=1))
-        plane_pool = ctx.enter_context(tc.tile_pool(name="planes", bufs=2 * IN_ROWS))
+        plane_pool = ctx.enter_context(tc.tile_pool(name="planes", bufs=4))
         grouped_pool = ctx.enter_context(tc.tile_pool(name="grouped", bufs=3))
         result_pool = ctx.enter_context(tc.tile_pool(name="result", bufs=8))
         turned_pool = ctx.enter_context(tc.psum_pool(name="turned", bufs=IN_ROWS))
@@ -73,7 +72,7 @@ def tile_blockrf_t_e_kernel(
             ("beta", beta),
         ):
             raw[name] = keep.tile([P, PACK], BF16, name="raw_" + name)
-            nc.scalar.dma_start(out=raw[name][:], in_=vector.rearrange("(p t) -> p t", t=PACK))
+            nc.sync.dma_start(out=raw[name][:], in_=vector.rearrange("(p t) -> p t", t=PACK))
 
         def load_x(j):
             nc.sync.dma_start(out=x_sb[:, j, :], in_=x_dram[j])
@@ -87,19 +86,22 @@ def tile_blockrf_t_e_kernel(
         nc.vector.memset(w_planes[:].bitcast(I32), 0)
         make_identity(nc, identity[:])
 
-        for j in range(AHEAD + 1):
-            load_x(j)
-        load_weight_words(0)
-        for block in range(WEIGHT_GROUPS // PLANES_PER_TILE):
+        def load_weight_scales(block):
             groups = slice(PLANES_PER_TILE * block, PLANES_PER_TILE * (block + 1))
             for quadrant in range(4):
                 nc.sync.dma_start(
                     out=w_planes[32 * quadrant : 32 * quadrant + 16, block, :].bitcast(I32),
                     in_=scales_dram[groups, 4 * quadrant : 4 * quadrant + 4, :],
                 )
-        for e in range(1, OUT_ROWS * WIDTH):
-            load_weight_words(e)
-        for j in range(AHEAD + 1, BATCH_TILES):
+
+        for j in range(FIRST_TILES):
+            load_x(j)
+        for h in range(OUT_ROWS):
+            load_weight_words(WIDTH * h)
+            load_weight_scales(h)
+            load_weight_words(WIDTH * h + 1)
+            load_x(FIRST_TILES + h)
+        for j in range(FIRST_TILES + OUT_ROWS, BATCH_TILES):
             load_x(j)
 
         def small(name):
@@ -177,15 +179,7 @@ def tile_blockrf_t_e_kernel(
                 in_=grouped[j, h][:].rearrange("p c t -> p (c t)"),
             )
 
-        def quantise_tile(j):
-            for h in range(IN_ROWS + 1):
-                if h < IN_ROWS:
-                    regroup(j, h)
-                if h >= 1:
-                    quantise(j, h - 1)
-
-        def multiply(j, bank):
-            e, half = divmod(bank, HALVES)
+        def multiply(j, e, half, on_scalar):
             h, w = divmod(e, WIDTH)
             f_cols = slice(half * N_HALF, (half + 1) * N_HALF)
             acc = acc_pool.tile([P, N_HALF], F32, name="acc")
@@ -206,22 +200,52 @@ def tile_blockrf_t_e_kernel(
                 )
             if w == 0 and half == 0:
                 result[j, h] = result_pool.tile([P, WIDTH, FEATURES], F32, name="result")
-            if bank % 3 == 0:
+            if on_scalar:
                 nc.scalar.activation(out=result[j, h][:, w, f_cols], in_=acc[:], func=ACT.Relu)
             else:
                 nc.vector.tensor_scalar_max(result[j, h][:, w, f_cols], acc[:], 0.0)
-            if w == WIDTH - 1 and half == HALVES - 1:
+            if half < HALVES - 1:
+                return
+            if j == BATCH_TILES - 1:
+                nc.sync.dma_start(
+                    out=out_dram[j, :, h, w * FEATURES : (w + 1) * FEATURES],
+                    in_=result[j, h][:, w, :],
+                )
+            elif w == WIDTH - 1:
                 nc.sync.dma_start(
                     out=out_dram[j, :, h, :], in_=result[j, h][:].rearrange("p w f -> p (w f)")
                 )
 
-        for s in range(BATCH_TILES + AHEAD):
-            if s < BATCH_TILES:
-                transpose_tile(s)
-            if 1 <= s <= BATCH_TILES:
-                quantise_tile(s - 1)
-            for bank in range(BANKS_PER_TILE):
-                if s < BATCH_TILES and bank % 3 == 0:
-                    batch_norm(s, bank // 3)
-                if s >= AHEAD:
-                    multiply(s - AHEAD, bank)
+        def step(banks, next_tile):
+            prepare = next_tile < BATCH_TILES
+            for row in range(IN_ROWS):
+                if prepare:
+                    batch_norm(next_tile, row)
+                if 3 * row < len(banks):
+                    multiply(*banks[3 * row], on_scalar=True)
+                if prepare:
+                    regroup(next_tile, row)
+                if 3 * row + 1 < len(banks):
+                    multiply(*banks[3 * row + 1], on_scalar=False)
+                if prepare:
+                    quantise(next_tile, row)
+                if 3 * row + 2 < len(banks):
+                    multiply(*banks[3 * row + 2], on_scalar=False)
+
+        for j in range(FIRST_TILES):
+            transpose_tile(j)
+            step([], j)
+        for h in range(OUT_ROWS):
+            banks = [
+                (j, WIDTH * h + w, half)
+                for j in range(FIRST_TILES)
+                for w in range(WIDTH)
+                for half in range(HALVES)
+            ]
+            step(banks, FIRST_TILES if h == OUT_ROWS - 1 else BATCH_TILES)
+            transpose_tile(FIRST_TILES + h)
+        for j in range(FIRST_TILES, BATCH_TILES):
+            banks = [(j, e, half) for e in range(OUT_ROWS * WIDTH) for half in range(HALVES)]
+            step(banks, j + 1)
+            if j + 2 < BATCH_TILES:
+                transpose_tile(j + 2)

@@ -48,8 +48,8 @@ def tile_blockrf_t_e_kernel(
 
     with ExitStack() as ctx:
         keep = ctx.enter_context(tc.tile_pool(name="keep", bufs=1))
-        plane_pool = ctx.enter_context(tc.tile_pool(name="planes", bufs=4))
-        grouped_pool = ctx.enter_context(tc.tile_pool(name="grouped", bufs=3))
+        plane_pool = ctx.enter_context(tc.tile_pool(name="planes", bufs=2 * IN_ROWS))
+        grouped_pool = ctx.enter_context(tc.tile_pool(name="grouped", bufs=IN_ROWS + 1))
         result_pool = ctx.enter_context(tc.tile_pool(name="result", bufs=8))
         turned_pool = ctx.enter_context(tc.psum_pool(name="turned", bufs=IN_ROWS))
         acc_pool = ctx.enter_context(tc.psum_pool(name="acc", bufs=8 - IN_ROWS))
@@ -154,22 +154,42 @@ def tile_blockrf_t_e_kernel(
             planes[j, h] = plane_pool.tile([P, PACK, ROW_COLS], BF16, name="planes")
             halves = turned[j, h][:].bitcast(BF16).rearrange("p u (c e) -> p u c e", e=2)
             for t in range(PACK):
-                nc.scalar.activation(
-                    out=planes[j, h][:, t, :],
-                    in_=halves[:, t // 2, :, t % 2],
-                    func=ACT.Identity,
-                    scale=bn_scale[:, t : t + 1],
-                    bias=bn_shift[:, t : t + 1],
-                )
+                if h % 2 == 0:
+                    nc.scalar.activation(
+                        out=planes[j, h][:, t, :],
+                        in_=halves[:, t // 2, :, t % 2],
+                        func=ACT.Identity,
+                        scale=bn_scale[:, t : t + 1],
+                        bias=bn_shift[:, t : t + 1],
+                    )
+                else:
+                    nc.vector.tensor_scalar(
+                        out=planes[j, h][:, t, :],
+                        in0=halves[:, t // 2, :, t % 2],
+                        scalar1=bn_scale[:, t : t + 1],
+                        scalar2=bn_shift[:, t : t + 1],
+                        op0=ALU.mult,
+                        op1=ALU.add,
+                    )
 
         def regroup(j, h):
             grouped[j, h] = grouped_pool.tile(
                 [P, ROW_COLS, PACK], BF16, name="grouped", align_bytes=64
             )
-            nc.vector.tensor_copy(
-                out=grouped[j, h][:].rearrange("p (c i) t -> p c t i", i=4),
-                in_=planes[j, h][:].rearrange("p t (c i) -> p c t i", i=4),
-            )
+            if j < FIRST_TILES:
+                nc.vector.tensor_copy(
+                    out=grouped[j, h][:].rearrange("p (c i) t -> p c t i", i=4),
+                    in_=planes[j, h][:].rearrange("p t (c i) -> p c t i", i=4),
+                )
+            else:
+                nc.gpsimd.tensor_scalar(
+                    out=grouped[j, h][:],
+                    in0=planes[j, h][:].rearrange("p t c -> p c t"),
+                    scalar1=1.0,
+                    scalar2=0.0,
+                    op0=ALU.mult,
+                    op1=ALU.add,
+                )
 
         def quantise(j, h):
             cols = slice(h * ROW_COLS, (h + 1) * ROW_COLS)
@@ -216,25 +236,27 @@ def tile_blockrf_t_e_kernel(
                     out=out_dram[j, :, h, :], in_=result[j, h][:].rearrange("p w f -> p (w f)")
                 )
 
-        def step(banks, next_tile):
-            prepare = next_tile < BATCH_TILES
-            for row in range(IN_ROWS):
-                if prepare:
-                    batch_norm(next_tile, row)
-                if 3 * row < len(banks):
-                    multiply(*banks[3 * row], on_scalar=True)
-                if prepare:
-                    regroup(next_tile, row)
-                if 3 * row + 1 < len(banks):
-                    multiply(*banks[3 * row + 1], on_scalar=False)
-                if prepare:
-                    quantise(next_tile, row)
-                if 3 * row + 2 < len(banks):
-                    multiply(*banks[3 * row + 2], on_scalar=False)
+        def normalise_tile(j):
+            for h in range(IN_ROWS):
+                batch_norm(j, h)
+            for h in range(IN_ROWS):
+                regroup(j, h)
+
+        def multiply_banks(banks, next_tile):
+            for k in range(len(banks)):
+                multiply(*banks[k], on_scalar=(k % 2 == 0))
+                if next_tile < BATCH_TILES and k % 2 == 1 and k // 2 < IN_ROWS:
+                    quantise(next_tile, k // 2)
 
         for j in range(FIRST_TILES):
             transpose_tile(j)
-            step([], j)
+            for h in range(IN_ROWS):
+                batch_norm(j, h)
+            for h in range(IN_ROWS + 1):
+                if h < IN_ROWS:
+                    regroup(j, h)
+                if h >= 1:
+                    quantise(j, h - 1)
         for h in range(OUT_ROWS):
             banks = [
                 (j, WIDTH * h + w, half)
@@ -242,10 +264,15 @@ def tile_blockrf_t_e_kernel(
                 for w in range(WIDTH)
                 for half in range(HALVES)
             ]
-            step(banks, FIRST_TILES if h == OUT_ROWS - 1 else BATCH_TILES)
+            next_tile = FIRST_TILES if h == OUT_ROWS - 1 else BATCH_TILES
+            if next_tile < BATCH_TILES:
+                normalise_tile(next_tile)
+            multiply_banks(banks, next_tile)
             transpose_tile(FIRST_TILES + h)
         for j in range(FIRST_TILES, BATCH_TILES):
             banks = [(j, e, half) for e in range(OUT_ROWS * WIDTH) for half in range(HALVES)]
-            step(banks, j + 1)
+            if j + 1 < BATCH_TILES:
+                normalise_tile(j + 1)
+            multiply_banks(banks, j + 1)
             if j + 2 < BATCH_TILES:
                 transpose_tile(j + 2)

@@ -48,8 +48,8 @@ def tile_blockrf_t_e_kernel(
 
     with ExitStack() as ctx:
         keep = ctx.enter_context(tc.tile_pool(name="keep", bufs=1))
-        plane_pool = ctx.enter_context(tc.tile_pool(name="planes", bufs=2 * IN_ROWS))
-        grouped_pool = ctx.enter_context(tc.tile_pool(name="grouped", bufs=IN_ROWS + 1))
+        plane_pool = ctx.enter_context(tc.tile_pool(name="planes", bufs=4))
+        grouped_pool = ctx.enter_context(tc.tile_pool(name="grouped", bufs=3))
         result_pool = ctx.enter_context(tc.tile_pool(name="result", bufs=8))
         turned_pool = ctx.enter_context(tc.psum_pool(name="turned", bufs=IN_ROWS))
         acc_pool = ctx.enter_context(tc.psum_pool(name="acc", bufs=8 - IN_ROWS))
@@ -94,7 +94,11 @@ def tile_blockrf_t_e_kernel(
                     in_=scales_dram[groups, 4 * quadrant : 4 * quadrant + 4, :],
                 )
 
-        for j in range(FIRST_TILES):
+        row_elems = WIDTH * CHANNELS
+        for h in range(IN_ROWS):
+            elems = slice(h * row_elems, (h + 1) * row_elems)
+            nc.sync.dma_start(out=x_sb[:, 0, elems], in_=x_dram[0][:, elems])
+        for j in range(1, FIRST_TILES):
             load_x(j)
         for h in range(OUT_ROWS):
             load_weight_words(WIDTH * h)
@@ -111,22 +115,33 @@ def tile_blockrf_t_e_kernel(
         nc.vector.tensor_scalar_add(var_eps[:], raw["var"][:], BN_EPS)
         std = small("std")
         nc.scalar.activation(out=std[:], in_=var_eps[:], func=ACT.Sqrt)
-        rstd = small("rstd")
-        nc.vector.reciprocal(rstd[:], std[:])
-        r_sq = small("r_sq")
-        nc.vector.tensor_mul(r_sq[:], rstd[:], rstd[:])
-        v_r_sq = small("v_r_sq")
-        nc.vector.tensor_mul(v_r_sq[:], r_sq[:], var_eps[:])
-        factor = small("factor")
-        nc.vector.tensor_scalar(
-            out=factor[:], in0=v_r_sq[:], scalar1=-0.5, scalar2=1.5, op0=ALU.mult, op1=ALU.add
+        inv_var = small("inv_var")
+        nc.vector.reciprocal(inv_var[:], var_eps[:])
+        gamma_over_var = small("gamma_over_var")
+        nc.vector.tensor_mul(gamma_over_var[:], raw["gamma"][:], inv_var[:])
+        std_sq = small("std_sq")
+        nc.vector.tensor_mul(std_sq[:], std[:], std[:])
+        gamma_r = small("gamma_r")
+        nc.vector.tensor_mul(gamma_r[:], gamma_over_var[:], std[:])
+        newton = small("newton")
+        nc.vector.scalar_tensor_tensor(
+            out=newton[:], in0=std_sq[:], scalar=-0.5, in1=inv_var[:], op0=ALU.mult, op1=ALU.mult
         )
-        rstd_fine = small("rstd_fine")
-        nc.vector.tensor_mul(rstd_fine[:], rstd[:], factor[:])
+        mean_gamma_r = small("mean_gamma_r")
+        nc.vector.tensor_mul(mean_gamma_r[:], raw["mean"][:], gamma_r[:])
         bn_scale = small("bn_scale")
-        nc.vector.tensor_mul(bn_scale[:], raw["gamma"][:], rstd_fine[:])
+        nc.vector.scalar_tensor_tensor(
+            out=bn_scale[:], in0=newton[:], scalar=1.5, in1=gamma_r[:], op0=ALU.add, op1=ALU.mult
+        )
         mean_scaled = small("mean_scaled")
-        nc.vector.tensor_mul(mean_scaled[:], raw["mean"][:], bn_scale[:])
+        nc.vector.scalar_tensor_tensor(
+            out=mean_scaled[:],
+            in0=newton[:],
+            scalar=1.5,
+            in1=mean_gamma_r[:],
+            op0=ALU.add,
+            op1=ALU.mult,
+        )
         bn_shift = small("bn_shift")
         nc.vector.tensor_sub(bn_shift[:], raw["beta"][:], mean_scaled[:])
 
@@ -154,42 +169,22 @@ def tile_blockrf_t_e_kernel(
             planes[j, h] = plane_pool.tile([P, PACK, ROW_COLS], BF16, name="planes")
             halves = turned[j, h][:].bitcast(BF16).rearrange("p u (c e) -> p u c e", e=2)
             for t in range(PACK):
-                if h % 2 == 0:
-                    nc.scalar.activation(
-                        out=planes[j, h][:, t, :],
-                        in_=halves[:, t // 2, :, t % 2],
-                        func=ACT.Identity,
-                        scale=bn_scale[:, t : t + 1],
-                        bias=bn_shift[:, t : t + 1],
-                    )
-                else:
-                    nc.vector.tensor_scalar(
-                        out=planes[j, h][:, t, :],
-                        in0=halves[:, t // 2, :, t % 2],
-                        scalar1=bn_scale[:, t : t + 1],
-                        scalar2=bn_shift[:, t : t + 1],
-                        op0=ALU.mult,
-                        op1=ALU.add,
-                    )
+                nc.scalar.activation(
+                    out=planes[j, h][:, t, :],
+                    in_=halves[:, t // 2, :, t % 2],
+                    func=ACT.Identity,
+                    scale=bn_scale[:, t : t + 1],
+                    bias=bn_shift[:, t : t + 1],
+                )
 
         def regroup(j, h):
             grouped[j, h] = grouped_pool.tile(
                 [P, ROW_COLS, PACK], BF16, name="grouped", align_bytes=64
             )
-            if j < FIRST_TILES:
-                nc.vector.tensor_copy(
-                    out=grouped[j, h][:].rearrange("p (c i) t -> p c t i", i=4),
-                    in_=planes[j, h][:].rearrange("p t (c i) -> p c t i", i=4),
-                )
-            else:
-                nc.gpsimd.tensor_scalar(
-                    out=grouped[j, h][:],
-                    in0=planes[j, h][:].rearrange("p t c -> p c t"),
-                    scalar1=1.0,
-                    scalar2=0.0,
-                    op0=ALU.mult,
-                    op1=ALU.add,
-                )
+            nc.vector.tensor_copy(
+                out=grouped[j, h][:].rearrange("p (c i) t -> p c t i", i=4),
+                in_=planes[j, h][:].rearrange("p t (c i) -> p c t i", i=4),
+            )
 
         def quantise(j, h):
             cols = slice(h * ROW_COLS, (h + 1) * ROW_COLS)
@@ -236,43 +231,35 @@ def tile_blockrf_t_e_kernel(
                     out=out_dram[j, :, h, :], in_=result[j, h][:].rearrange("p w f -> p (w f)")
                 )
 
-        def normalise_tile(j):
-            for h in range(IN_ROWS):
-                batch_norm(j, h)
-            for h in range(IN_ROWS):
-                regroup(j, h)
-
-        def multiply_banks(banks, next_tile):
-            for k in range(len(banks)):
-                multiply(*banks[k], on_scalar=(k % 2 == 0))
-                if next_tile < BATCH_TILES and k % 2 == 1 and k // 2 < IN_ROWS:
-                    quantise(next_tile, k // 2)
+        def step(banks, next_tile):
+            prepare = next_tile < BATCH_TILES
+            for row in range(IN_ROWS):
+                if prepare:
+                    batch_norm(next_tile, row)
+                if 3 * row < len(banks):
+                    multiply(*banks[3 * row], on_scalar=True)
+                if prepare:
+                    regroup(next_tile, row)
+                if 3 * row + 1 < len(banks):
+                    multiply(*banks[3 * row + 1], on_scalar=False)
+                if prepare:
+                    quantise(next_tile, row)
+                if 3 * row + 2 < len(banks):
+                    multiply(*banks[3 * row + 2], on_scalar=False)
 
         for j in range(FIRST_TILES):
             transpose_tile(j)
-            for h in range(IN_ROWS):
-                batch_norm(j, h)
-            for h in range(IN_ROWS + 1):
-                if h < IN_ROWS:
-                    regroup(j, h)
-                if h >= 1:
-                    quantise(j, h - 1)
-        for h in range(OUT_ROWS):
-            banks = [
-                (j, WIDTH * h + w, half)
-                for j in range(FIRST_TILES)
-                for w in range(WIDTH)
-                for half in range(HALVES)
-            ]
-            next_tile = FIRST_TILES if h == OUT_ROWS - 1 else BATCH_TILES
-            if next_tile < BATCH_TILES:
-                normalise_tile(next_tile)
-            multiply_banks(banks, next_tile)
-            transpose_tile(FIRST_TILES + h)
+            step([], j)
+        def row_banks(j, h):
+            return [(j, WIDTH * h + w, half) for w in range(WIDTH) for half in range(HALVES)]
+
+        step(row_banks(0, 0), BATCH_TILES)
+        transpose_tile(FIRST_TILES)
+        step(row_banks(1, 0), BATCH_TILES)
+        step(row_banks(0, 1) + row_banks(1, 1), FIRST_TILES)
+        transpose_tile(FIRST_TILES + 1)
         for j in range(FIRST_TILES, BATCH_TILES):
             banks = [(j, e, half) for e in range(OUT_ROWS * WIDTH) for half in range(HALVES)]
-            if j + 1 < BATCH_TILES:
-                normalise_tile(j + 1)
-            multiply_banks(banks, j + 1)
+            step(banks, j + 1)
             if j + 2 < BATCH_TILES:
                 transpose_tile(j + 2)

@@ -32,6 +32,7 @@ HALVES = FEATURES // N_HALF
 WEIGHT_GROUPS = OUT_ROWS * WIDTH * WINDOW
 PLANES_PER_TILE = 4
 FIRST_TILES = 2
+FIRST_SORTED = 3
 
 FLOPS = 2 * BATCH * OUT_ROWS * WIDTH * WINDOW * CHANNELS * FEATURES
 
@@ -50,6 +51,7 @@ def tile_blockrf_t_e_kernel(
         keep = ctx.enter_context(tc.tile_pool(name="keep", bufs=1))
         plane_pool = ctx.enter_context(tc.tile_pool(name="planes", bufs=4))
         grouped_pool = ctx.enter_context(tc.tile_pool(name="grouped", bufs=3))
+        sorted_pool = ctx.enter_context(tc.tile_pool(name="sorted", bufs=2))
         result_pool = ctx.enter_context(tc.tile_pool(name="result", bufs=8))
         turned_pool = ctx.enter_context(tc.psum_pool(name="turned", bufs=IN_ROWS))
         acc_pool = ctx.enter_context(tc.psum_pool(name="acc", bufs=8 - IN_ROWS))
@@ -145,10 +147,20 @@ def tile_blockrf_t_e_kernel(
         bn_shift = small("bn_shift")
         nc.vector.tensor_sub(bn_shift[:], raw["beta"][:], mean_scaled[:])
 
+        sorted_words = {}
         turned = {}
         planes = {}
         grouped = {}
         result = {}
+
+        def sort_words(j):
+            sorted_words[j] = sorted_pool.tile(
+                [P, IN_ROWS * WIDTH, 2, P], F32, name="sorted_words"
+            )
+            nc.vector.tensor_copy(
+                out=sorted_words[j][:],
+                in_=x_sb[:, j, :].bitcast(F32).rearrange("b (x p u) -> b x u p", p=P, u=2),
+            )
 
         def transpose_tile(j):
             x_as_words = x_sb[:, j, :].bitcast(F32)
@@ -157,11 +169,15 @@ def tile_blockrf_t_e_kernel(
                 for w in range(WIDTH):
                     pixel = h * WIDTH + w
                     for u in range(2):
+                        if j < FIRST_SORTED:
+                            words = x_as_words[
+                                :, pixel * WORDS_PER_PIXEL + u : (pixel + 1) * WORDS_PER_PIXEL : 2
+                            ]
+                        else:
+                            words = sorted_words[j][:, pixel, u, :]
                         nc.tensor.transpose(
                             out=turned[j, h][:, u, w * P : (w + 1) * P],
-                            in_=x_as_words[
-                                :, pixel * WORDS_PER_PIXEL + u : (pixel + 1) * WORDS_PER_PIXEL : 2
-                            ],
+                            in_=words,
                             identity=identity[:],
                         )
 
@@ -231,21 +247,23 @@ def tile_blockrf_t_e_kernel(
                     out=out_dram[j, :, h, :], in_=result[j, h][:].rearrange("p w f -> p (w f)")
                 )
 
-        def step(banks, next_tile):
+        def step(banks, next_tile, sort_at=0):
             prepare = next_tile < BATCH_TILES
-            for row in range(IN_ROWS):
-                if prepare:
+            sort = FIRST_SORTED <= next_tile + 1 < BATCH_TILES
+            for n in range(max(len(banks), 2 * IN_ROWS + 2)):
+                row = n // 2
+                if sort and n == sort_at:
+                    sort_words(next_tile + 1)
+                if prepare and n % 2 == 0 and row < IN_ROWS:
                     batch_norm(next_tile, row)
-                if 3 * row < len(banks):
-                    multiply(*banks[3 * row], on_scalar=True)
-                if prepare:
-                    regroup(next_tile, row)
-                if 3 * row + 1 < len(banks):
-                    multiply(*banks[3 * row + 1], on_scalar=False)
-                if prepare:
-                    quantise(next_tile, row)
-                if 3 * row + 2 < len(banks):
-                    multiply(*banks[3 * row + 2], on_scalar=False)
+                if prepare and n % 2 == 0 and 1 <= row:
+                    if row >= 2:
+                        quantise(next_tile, row - 2)
+                    regroup(next_tile, row - 1)
+                if n < len(banks):
+                    multiply(*banks[n], on_scalar=(n % 2 == 0))
+            if prepare:
+                quantise(next_tile, IN_ROWS - 1)
 
         for j in range(FIRST_TILES):
             transpose_tile(j)
@@ -256,7 +274,7 @@ def tile_blockrf_t_e_kernel(
         step(row_banks(0, 0), BATCH_TILES)
         transpose_tile(FIRST_TILES)
         step(row_banks(1, 0), BATCH_TILES)
-        step(row_banks(0, 1) + row_banks(1, 1), FIRST_TILES)
+        step(row_banks(0, 1) + row_banks(1, 1), FIRST_TILES, sort_at=4)
         transpose_tile(FIRST_TILES + 1)
         for j in range(FIRST_TILES, BATCH_TILES):
             banks = [(j, e, half) for e in range(OUT_ROWS * WIDTH) for half in range(HALVES)]

@@ -74,7 +74,7 @@ def tile_blockrf_t_e_kernel(
             ("beta", beta),
         ):
             raw[name] = keep.tile([P, PACK], BF16, name="raw_" + name)
-            nc.sync.dma_start(out=raw[name][:], in_=vector.rearrange("(p t) -> p t", t=PACK))
+            nc.scalar.dma_start(out=raw[name][:], in_=vector.rearrange("(p t) -> p t", t=PACK))
 
         def load_x(j):
             nc.sync.dma_start(out=x_sb[:, j, :], in_=x_dram[j])

@@ -34,6 +34,8 @@ PLANES_PER_TILE = 4
 FIRST_TILES = 2
 FIRST_SORTED = 3
 
+WHOLE_STORES = 4
+JOINT_LOAD = 5
 FLOPS = 2 * BATCH * OUT_ROWS * WIDTH * WINDOW * CHANNELS * FEATURES
 
 
@@ -43,7 +45,7 @@ def tile_blockrf_t_e_kernel(
     nc = tc.nc
 
     x_dram = x.rearrange("(j p) h w c -> j p (h w c)", p=P)
-    out_dram = out.rearrange("(j p) h w f -> j p h (w f)", p=P)
+    out_dram = out.rearrange("(j p) h w f -> j p (h w f)", p=P)
     words_dram = weight_words.rearrange("g p n t -> p g (n t)").bitcast(I32)
     scales_dram = weight_scales.bitcast(I32)
 
@@ -52,7 +54,7 @@ def tile_blockrf_t_e_kernel(
         plane_pool = ctx.enter_context(tc.tile_pool(name="planes", bufs=4))
         grouped_pool = ctx.enter_context(tc.tile_pool(name="grouped", bufs=3))
         sorted_pool = ctx.enter_context(tc.tile_pool(name="sorted", bufs=2))
-        result_pool = ctx.enter_context(tc.tile_pool(name="result", bufs=8))
+        result_pool = ctx.enter_context(tc.tile_pool(name="result", bufs=4))
         turned_pool = ctx.enter_context(tc.psum_pool(name="turned", bufs=IN_ROWS))
         acc_pool = ctx.enter_context(tc.psum_pool(name="acc", bufs=8 - IN_ROWS))
         ctx.enter_context(tc.manual_schedule())
@@ -107,8 +109,11 @@ def tile_blockrf_t_e_kernel(
             load_weight_scales(h)
             load_weight_words(WIDTH * h + 1)
             load_x(FIRST_TILES + h)
-        for j in range(FIRST_TILES + OUT_ROWS, BATCH_TILES):
+        for j in range(FIRST_TILES + OUT_ROWS, JOINT_LOAD):
             load_x(j)
+        nc.sync.dma_start(
+            out=x_sb[:, JOINT_LOAD:, :], in_=x_dram[JOINT_LOAD:].rearrange("j p c -> p j c")
+        )
 
         def small(name):
             return keep.tile([P, PACK], F32, name=name)
@@ -210,6 +215,13 @@ def tile_blockrf_t_e_kernel(
                 in_=grouped[j, h][:].rearrange("p c t -> p (c t)"),
             )
 
+        def store_pixels(j):
+            if j < WHOLE_STORES:
+                return OUT_ROWS * WIDTH
+            if j < BATCH_TILES - 1:
+                return WIDTH
+            return 1
+
         def multiply(j, e, half, on_scalar):
             h, w = divmod(e, WIDTH)
             f_cols = slice(half * N_HALF, (half + 1) * N_HALF)
@@ -229,22 +241,20 @@ def tile_blockrf_t_e_kernel(
                     start=(i == 0),
                     stop=(i == WINDOW - 1),
                 )
-            if w == 0 and half == 0:
-                result[j, h] = result_pool.tile([P, WIDTH, FEATURES], F32, name="result")
+            if e == 0 and half == 0:
+                result[j] = result_pool.tile([P, OUT_ROWS * WIDTH, FEATURES], F32, name="result")
             if on_scalar:
-                nc.scalar.activation(out=result[j, h][:, w, f_cols], in_=acc[:], func=ACT.Relu)
+                nc.scalar.activation(out=result[j][:, e, f_cols], in_=acc[:], func=ACT.Relu)
             else:
-                nc.vector.tensor_scalar_max(result[j, h][:, w, f_cols], acc[:], 0.0)
+                nc.vector.tensor_scalar_max(result[j][:, e, f_cols], acc[:], 0.0)
             if half < HALVES - 1:
                 return
-            if j == BATCH_TILES - 1:
+            pixels = store_pixels(j)
+            if (e + 1) % pixels == 0:
+                first = e + 1 - pixels
                 nc.sync.dma_start(
-                    out=out_dram[j, :, h, w * FEATURES : (w + 1) * FEATURES],
-                    in_=result[j, h][:, w, :],
-                )
-            elif w == WIDTH - 1:
-                nc.sync.dma_start(
-                    out=out_dram[j, :, h, :], in_=result[j, h][:].rearrange("p w f -> p (w f)")
+                    out=out_dram[j, :, first * FEATURES : (e + 1) * FEATURES],
+                    in_=result[j][:, first : e + 1, :].rearrange("p e f -> p (e f)"),
                 )
 
         def step(banks, next_tile, sort_at=0):

@@ -60,12 +60,15 @@ def tile_blockrf_t_e_kernel(
         ctx.enter_context(tc.manual_schedule())
 
         x_sb = keep.tile([P, BATCH_TILES, IN_ROWS * WIDTH * CHANNELS], BF16)
-        w_words = keep.tile([P, WEIGHT_GROUPS, FEATURES], U32, align_bytes=64)
-        w_planes = keep.tile(
-            [P, WEIGHT_GROUPS // PLANES_PER_TILE, FEATURES], U8, align_bytes=64
+        w_words = keep.tile([P, WEIGHT_GROUPS, FEATURES], U32, align_bytes=256)
+        w_planes_room = keep.tile(
+            [P, 64 + WEIGHT_GROUPS // PLANES_PER_TILE * FEATURES], U8, align_bytes=256
         )
-        x_codes = keep.tile([P, BATCH_TILES, TILE_COLS], U32, align_bytes=64)
-        x_scales = keep.tile([P, BATCH_TILES, TILE_COLS], U8, align_bytes=64)
+        w_planes = w_planes_room[:, 64:].rearrange("p (z f) -> p z f", f=FEATURES)
+        x_codes_room = keep.tile([P, 32 + BATCH_TILES * TILE_COLS], U32, align_bytes=256)
+        x_codes = x_codes_room[:, 32:].rearrange("p (j c) -> p j c", c=TILE_COLS)
+        x_scales_room = keep.tile([P, 192 + BATCH_TILES * TILE_COLS], U8, align_bytes=256)
+        x_scales = x_scales_room[:, 192:].rearrange("p (j c) -> p j c", c=TILE_COLS)
         identity = keep.tile([P, P], F32)
 
         raw = {}
@@ -87,7 +90,7 @@ def tile_blockrf_t_e_kernel(
                 out=w_words[:, groups, :].bitcast(I32), in_=words_dram[:, groups, :]
             )
 
-        nc.vector.memset(w_planes[:].bitcast(I32), 0)
+        nc.vector.memset(w_planes_room[:].bitcast(I32), 0)
         make_identity(nc, identity[:])
 
         def load_weight_scales(block):

from contextlib import ExitStack

import concourse.mybir as mybir
from concourse.masks import make_identity

F32 = mybir.dt.float32
BF16 = mybir.dt.bfloat16
I32 = mybir.dt.int32
U32 = mybir.dt.uint32
U8 = mybir.dt.uint8
FP8X4 = mybir.dt.float8_e4m3fn_x4
ACT = mybir.ActivationFunctionType
ALU = mybir.AluOpType

P = 128
PACK = 4
BATCH = 1024
IN_ROWS = 3
OUT_ROWS = 2
WIDTH = 2
WINDOW = 2
CHANNELS = P * PACK
FEATURES = 1024
BN_EPS = 1e-3

BATCH_TILES = BATCH // P
ROW_COLS = WIDTH * P
TILE_COLS = IN_ROWS * ROW_COLS
WORDS_PER_PIXEL = CHANNELS // 2
N_HALF = 512
HALVES = FEATURES // N_HALF
WEIGHT_GROUPS = OUT_ROWS * WIDTH * WINDOW
PLANES_PER_TILE = 4
FIRST_TILES = 2
FIRST_SORTED = 3

WHOLE_STORES = 4
JOINT_LOAD = 5
FLOPS = 2 * BATCH * OUT_ROWS * WIDTH * WINDOW * CHANNELS * FEATURES


def tile_blockrf_t_e_kernel(
    tc, x, gamma, beta, moving_mean, moving_var, weight_words, weight_scales, out
):
    nc = tc.nc

    x_dram = x.rearrange("(j p) h w c -> j p (h w c)", p=P)
    out_dram = out.rearrange("(j p) h w f -> j p (h w f)", p=P)
    words_dram = weight_words.rearrange("g p n t -> p g (n t)").bitcast(I32)
    scales_dram = weight_scales.bitcast(I32)

    with ExitStack() as ctx:
        keep = ctx.enter_context(tc.tile_pool(name="keep", bufs=1))
        plane_pool = ctx.enter_context(tc.tile_pool(name="planes", bufs=4))
        grouped_pool = ctx.enter_context(tc.tile_pool(name="grouped", bufs=3))
        sorted_pool = ctx.enter_context(tc.tile_pool(name="sorted", bufs=2))
        result_pool = ctx.enter_context(tc.tile_pool(name="result", bufs=4))
        turned_pool = ctx.enter_context(tc.psum_pool(name="turned", bufs=IN_ROWS))
        acc_pool = ctx.enter_context(tc.psum_pool(name="acc", bufs=8 - IN_ROWS))
        ctx.enter_context(tc.manual_schedule())

        x_sb = keep.tile([P, BATCH_TILES, IN_ROWS * WIDTH * CHANNELS], BF16)
        w_words = keep.tile([P, WEIGHT_GROUPS, FEATURES], U32, align_bytes=256)
        w_planes_room = keep.tile(
            [P, 64 + WEIGHT_GROUPS // PLANES_PER_TILE * FEATURES], U8, align_bytes=256
        )
        w_planes = w_planes_room[:, 64:].rearrange("p (z f) -> p z f", f=FEATURES)
        x_codes_room = keep.tile([P, 32 + BATCH_TILES * TILE_COLS], U32, align_bytes=256)
        x_codes = x_codes_room[:, 32:].rearrange("p (j c) -> p j c", c=TILE_COLS)
        x_scales_room = keep.tile([P, 192 + BATCH_TILES * TILE_COLS], U8, align_bytes=256)
        x_scales = x_scales_room[:, 192:].rearrange("p (j c) -> p j c", c=TILE_COLS)
        identity = keep.tile([P, P], F32)

        raw = {}
        for name, vector in (
            ("var", moving_var),
            ("gamma", gamma),
            ("mean", moving_mean),
            ("beta", beta),
        ):
            raw[name] = keep.tile([P, PACK], BF16, name="raw_" + name)
            nc.scalar.dma_start(out=raw[name][:], in_=vector.rearrange("(p t) -> p t", t=PACK))

        def load_x(j):
            nc.sync.dma_start(out=x_sb[:, j, :], in_=x_dram[j])

        def load_weight_words(e):
            groups = slice(WINDOW * e, WINDOW * (e + 1))
            nc.sync.dma_start(
                out=w_words[:, groups, :].bitcast(I32), in_=words_dram[:, groups, :]
            )

        nc.vector.memset(w_planes_room[:].bitcast(I32), 0)
        make_identity(nc, identity[:])

        def load_weight_scales(block):
            groups = slice(PLANES_PER_TILE * block, PLANES_PER_TILE * (block + 1))
            for quadrant in range(4):
                nc.sync.dma_start(
                    out=w_planes[32 * quadrant : 32 * quadrant + 16, block, :].bitcast(I32),
                    in_=scales_dram[groups, 4 * quadrant : 4 * quadrant + 4, :],
                )

        row_elems = WIDTH * CHANNELS
        for h in range(IN_ROWS):
            elems = slice(h * row_elems, (h + 1) * row_elems)
            nc.sync.dma_start(out=x_sb[:, 0, elems], in_=x_dram[0][:, elems])
        for j in range(1, FIRST_TILES):
            load_x(j)
        for h in range(OUT_ROWS):
            load_weight_words(WIDTH * h)
            load_weight_scales(h)
            load_weight_words(WIDTH * h + 1)
            load_x(FIRST_TILES + h)
        for j in range(FIRST_TILES + OUT_ROWS, JOINT_LOAD):
            load_x(j)
        nc.sync.dma_start(
            out=x_sb[:, JOINT_LOAD:, :], in_=x_dram[JOINT_LOAD:].rearrange("j p c -> p j c")
        )

        def small(name):
            return keep.tile([P, PACK], F32, name=name)

        var_eps = small("var_eps")
        nc.vector.tensor_scalar_add(var_eps[:], raw["var"][:], BN_EPS)
        std = small("std")
        nc.scalar.activation(out=std[:], in_=var_eps[:], func=ACT.Sqrt)
        inv_var = small("inv_var")
        nc.vector.reciprocal(inv_var[:], var_eps[:])
        gamma_over_var = small("gamma_over_var")
        nc.vector.tensor_mul(gamma_over_var[:], raw["gamma"][:], inv_var[:])
        std_sq = small("std_sq")
        nc.vector.tensor_mul(std_sq[:], std[:], std[:])
        gamma_r = small("gamma_r")
        nc.vector.tensor_mul(gamma_r[:], gamma_over_var[:], std[:])
        newton = small("newton")
        nc.vector.scalar_tensor_tensor(
            out=newton[:], in0=std_sq[:], scalar=-0.5, in1=inv_var[:], op0=ALU.mult, op1=ALU.mult
        )
        mean_gamma_r = small("mean_gamma_r")
        nc.vector.tensor_mul(mean_gamma_r[:], raw["mean"][:], gamma_r[:])
        bn_scale = small("bn_scale")
        nc.vector.scalar_tensor_tensor(
            out=bn_scale[:], in0=newton[:], scalar=1.5, in1=gamma_r[:], op0=ALU.add, op1=ALU.mult
        )
        mean_scaled = small("mean_scaled")
        nc.vector.scalar_tensor_tensor(
            out=mean_scaled[:],
            in0=newton[:],
            scalar=1.5,
            in1=mean_gamma_r[:],
            op0=ALU.add,
            op1=ALU.mult,
        )
        bn_shift = small("bn_shift")
        nc.vector.tensor_sub(bn_shift[:], raw["beta"][:], mean_scaled[:])

        sorted_words = {}
        turned = {}
        planes = {}
        grouped = {}
        result = {}

        def sort_words(j):
            sorted_words[j] = sorted_pool.tile(
                [P, IN_ROWS * WIDTH, 2, P], F32, name="sorted_words"
            )
            nc.vector.tensor_copy(
                out=sorted_words[j][:],
                in_=x_sb[:, j, :].bitcast(F32).rearrange("b (x p u) -> b x u p", p=P, u=2),
            )

        def transpose_tile(j):
            x_as_words = x_sb[:, j, :].bitcast(F32)
            for h in range(IN_ROWS):
                turned[j, h] = turned_pool.tile([P, 2, ROW_COLS], F32, name="turned")
                for w in range(WIDTH):
                    pixel = h * WIDTH + w
                    for u in range(2):
                        if j < FIRST_SORTED:
                            words = x_as_words[
                                :, pixel * WORDS_PER_PIXEL + u : (pixel + 1) * WORDS_PER_PIXEL : 2
                            ]
                        else:
                            words = sorted_words[j][:, pixel, u, :]
                        nc.tensor.transpose(
                            out=turned[j, h][:, u, w * P : (w + 1) * P],
                            in_=words,
                            identity=identity[:],
                        )

        def batch_norm(j, h):
            planes[j, h] = plane_pool.tile([P, PACK, ROW_COLS], BF16, name="planes")
            halves = turned[j, h][:].bitcast(BF16).rearrange("p u (c e) -> p u c e", e=2)
            for t in range(PACK):
                nc.scalar.activation(
                    out=planes[j, h][:, t, :],
                    in_=halves[:, t // 2, :, t % 2],
                    func=ACT.Identity,
                    scale=bn_scale[:, t : t + 1],
                    bias=bn_shift[:, t : t + 1],
                )

        def regroup(j, h):
            grouped[j, h] = grouped_pool.tile(
                [P, ROW_COLS, PACK], BF16, name="grouped", align_bytes=64
            )
            nc.vector.tensor_copy(
                out=grouped[j, h][:].rearrange("p (c i) t -> p c t i", i=4),
                in_=planes[j, h][:].rearrange("p t (c i) -> p c t i", i=4),
            )

        def quantise(j, h):
            cols = slice(h * ROW_COLS, (h + 1) * ROW_COLS)
            nc.vector.quantize_mx(
                out=x_codes[:, j, cols].bitcast(FP8X4),
                scales=x_scales[:, j, cols],
                in_=grouped[j, h][:].rearrange("p c t -> p (c t)"),
            )

        def store_pixels(j):
            if j < WHOLE_STORES:
                return OUT_ROWS * WIDTH
            if j < BATCH_TILES - 1:
                return WIDTH
            return 1

        def multiply(j, e, half, on_scalar):
            h, w = divmod(e, WIDTH)
            f_cols = slice(half * N_HALF, (half + 1) * N_HALF)
            acc = acc_pool.tile([P, N_HALF], F32, name="acc")
            for i in range(WINDOW):
                g = WINDOW * e + i
                pixel = (h + i) * WIDTH + w
                b_cols = slice(pixel * P, (pixel + 1) * P)
                nc.tensor.matmul_mx(
                    out=acc[:],
                    lhsT=x_codes[:, j, b_cols].bitcast(FP8X4),
                    lhsT_scale=x_scales[:, j, b_cols],
                    rhs=w_words[:, g, f_cols].bitcast(FP8X4),
                    rhs_scale=w_planes[
                        4 * (g % PLANES_PER_TILE) : P, g // PLANES_PER_TILE, f_cols
                    ],
                    start=(i == 0),
                    stop=(i == WINDOW - 1),
                )
            if e == 0 and half == 0:
                result[j] = result_pool.tile([P, OUT_ROWS * WIDTH, FEATURES], F32, name="result")
            if on_scalar:
                nc.scalar.activation(out=result[j][:, e, f_cols], in_=acc[:], func=ACT.Relu)
            else:
                nc.vector.tensor_scalar_max(result[j][:, e, f_cols], acc[:], 0.0)
            if half < HALVES - 1:
                return
            pixels = store_pixels(j)
            if (e + 1) % pixels == 0:
                first = e + 1 - pixels
                nc.sync.dma_start(
                    out=out_dram[j, :, first * FEATURES : (e + 1) * FEATURES],
                    in_=result[j][:, first : e + 1, :].rearrange("p e f -> p (e f)"),
                )

        def step(banks, next_tile, sort_at=0):
            prepare = next_tile < BATCH_TILES
            sort = FIRST_SORTED <= next_tile + 1 < BATCH_TILES
            for n in range(max(len(banks), 2 * IN_ROWS + 2)):
                row = n // 2
                if sort and n == sort_at:
                    sort_words(next_tile + 1)
                if prepare and n % 2 == 0 and row < IN_ROWS:
                    batch_norm(next_tile, row)
                if prepare and n % 2 == 0 and 1 <= row:
                    if row >= 2:
                        quantise(next_tile, row - 2)
                    regroup(next_tile, row - 1)
                if n < len(banks):
                    multiply(*banks[n], on_scalar=(n % 2 == 0))
            if prepare:
                quantise(next_tile, IN_ROWS - 1)

        for j in range(FIRST_TILES):
            transpose_tile(j)
            step([], j)
        def row_banks(j, h):
            return [(j, WIDTH * h + w, half) for w in range(WIDTH) for half in range(HALVES)]

        step(row_banks(0, 0), BATCH_TILES)
        transpose_tile(FIRST_TILES)
        step(row_banks(1, 0), BATCH_TILES)
        step(row_banks(0, 1) + row_banks(1, 1), FIRST_TILES, sort_at=4)
        transpose_tile(FIRST_TILES + 1)
        for j in range(FIRST_TILES, BATCH_TILES):
            banks = [(j, e, half) for e in range(OUT_ROWS * WIDTH) for half in range(HALVES)]
            step(banks, j + 1)
            if j + 2 < BATCH_TILES:
                transpose_tile(j + 2)
